import numpy as np
import ml_dtypes


def mxq(x, axis, fmt="e4m3"):
    dtype, down = {"e4m3": (ml_dtypes.float8_e4m3fn, 7), "e5m2": (ml_dtypes.float8_e5m2, 14)}[fmt]
    v = np.moveaxis(np.asarray(x, np.float32).astype(ml_dtypes.bfloat16).astype(np.float64), axis, -1)
    blocks = v.reshape(v.shape[:-1] + (-1, 32))
    amax = np.abs(blocks).max(-1, keepdims=True)
    byte = np.maximum(np.where(amax > 0, np.frexp(amax)[1] - 1 + 127, 0) - down, 1)
    scale = np.exp2(byte - 127.0)
    codes = (blocks / scale).astype(np.float32).astype(dtype).astype(np.float64)
    return np.moveaxis((codes * scale).reshape(v.shape), -1, axis)


WIDE = False


def mx_kscale(k):
    if not WIDE:
        return np.ones(k)
    levels = np.array([20, -20, 10, -10, 0])
    a = np.random.permutation(np.resize(levels, k // 512 * 4)).reshape(k // 512, 4)
    idx = np.arange(k)
    return np.exp2(a[idx // 512, idx % 128 // 32])


BF16 = ml_dtypes.bfloat16


def bf(x):
    return np.asarray(x, np.float32).astype(BF16)


def f64(x):
    return np.asarray(x).astype(np.float64)


BATCH, IN_DIM, OUT_DIM = 16384, 512, 512
LN2 = np.log(2.0)


def setup_inputs():
    s = mx_kscale(BATCH)[:, None]
    x = np.random.standard_normal((BATCH, IN_DIM)) * (8.0 / np.sqrt(IN_DIM)) * s
    shift = np.random.randint(-10, 0, (IN_DIM, OUT_DIM))
    sign = np.random.randint(0, 2, (IN_DIM, OUT_DIM))
    bias = np.random.standard_normal((1, OUT_DIM)) * 0.5
    g = np.random.standard_normal((BATCH, OUT_DIM)) * np.exp2(np.random.randint(-12, 1, (BATCH, 1))) * 16.0 / s
    return {"x": bf(x), "shift": bf(shift), "sign": bf(sign), "bias": bf(bias), "grad_out": bf(g)}


def reference(x, shift, sign, bias, grad_out):
    dW = mxq(f64(x), 0, "e4m3").T @ mxq(f64(grad_out), 0, "e5m2")
    W = np.exp2(f64(shift)) * (1.0 - 2.0 * f64(sign))
    return dW * W * LN2

@@ -1,0 +1,119 @@
+from contextlib import ExitStack
+import math
+
+import concourse.mybir as mybir
+
+BF16 = mybir.dt.bfloat16
+F32 = mybir.dt.float32
+U32 = mybir.dt.uint32
+U8 = mybir.dt.uint8
+E4M3X4 = mybir.dt.float8_e4m3fn_x4
+E5M2X4 = mybir.dt.float8_e5m2_x4
+ALU = mybir.AluOpType
+ACT = mybir.ActivationFunctionType
+
+P = 128
+PACK = 4
+K_PASS = P * PACK
+TOKENS = 16384
+IN_DIM = 512
+OUT_DIM = 512
+M_TILES = IN_DIM // P
+PASSES = TOKENS // K_PASS
+LN2 = math.log(2.0)
+
+FLOPS = 2 * TOKENS * IN_DIM * OUT_DIM
+BYTES = 2 * TOKENS * (IN_DIM + OUT_DIM) + 2 * 2 * IN_DIM * OUT_DIM + 4 * IN_DIM * OUT_DIM
+
+
+def regroup(copy, grouped, raw):
+    copy(
+        out=grouped.rearrange("p (c i) t -> p c t i", i=4),
+        in_=raw.rearrange("p t (c i) -> p c t i", i=4),
+    )
+
+
+def tile_denseshift_kernel(tc, x, shift, sign, bias, grad_out, out):
+    nc = tc.nc
+    x_rows = x.rearrange("(c p j) w -> c p (j w)", p=P, j=PACK)
+    g_rows = grad_out.rearrange("(c p j) w -> c p (j w)", p=P, j=PACK)
+    with ExitStack() as ctx:
+        raw_pool = ctx.enter_context(tc.tile_pool(name="raw", bufs=8))
+        grp_pool = ctx.enter_context(tc.tile_pool(name="grp", bufs=3))
+        mx_pool = ctx.enter_context(tc.tile_pool(name="mx", bufs=4))
+        w_pool = ctx.enter_context(tc.tile_pool(name="w", bufs=1))
+        psum = ctx.enter_context(tc.psum_pool(name="acc", bufs=1))
+
+        warm = w_pool.tile([P, 1], F32)
+        nc.vector.memset(warm[:], 0.0)
+        nc.scalar.activation(out=warm[:], in_=warm[:], func=ACT.Exp)
+
+        acc = [psum.tile([P, OUT_DIM], F32, name="acc%d" % m) for m in range(M_TILES)]
+
+        shift_sb = w_pool.tile([P, M_TILES, OUT_DIM], BF16)
+        sign_sb = w_pool.tile([P, M_TILES, OUT_DIM], BF16)
+        pow2 = w_pool.tile([P, M_TILES, OUT_DIM], F32)
+        weight = w_pool.tile([P, M_TILES, OUT_DIM], F32)
+
+        for c in range(PASSES):
+            x_raw = raw_pool.tile([P, PACK, IN_DIM], BF16)
+            g_raw = raw_pool.tile([P, PACK, OUT_DIM], BF16)
+            nc.sync.dma_start(out=x_raw[:].rearrange("p j w -> p (j w)"), in_=x_rows[c])
+            nc.sync.dma_start(out=g_raw[:].rearrange("p j w -> p (j w)"), in_=g_rows[c])
+            if c == 1:
+                nc.sync.dma_start(out=shift_sb[:], in_=shift.rearrange("(m p) n -> p m n", p=P))
+                nc.sync.dma_start(out=sign_sb[:], in_=sign.rearrange("(m p) n -> p m n", p=P))
+
+            x_grp = grp_pool.tile([P, IN_DIM, PACK], BF16, align_bytes=64)
+            g_grp = grp_pool.tile([P, OUT_DIM, PACK], BF16, align_bytes=64)
+            regroup(nc.vector.tensor_copy, x_grp[:], x_raw[:])
+            regroup(nc.scalar.copy, g_grp[:], g_raw[:])
+
+            x_codes = mx_pool.tile([P, IN_DIM], U32, align_bytes=64)
+            x_scales = mx_pool.tile([P, IN_DIM], U8, align_bytes=64)
+            g_codes = mx_pool.tile([P, OUT_DIM], U32, align_bytes=64)
+            g_scales = mx_pool.tile([P, OUT_DIM], U8, align_bytes=64)
+            nc.vector.quantize_mx(
+                out=x_codes[:].bitcast(E4M3X4),
+                scales=x_scales[:],
+                in_=x_grp[:].rearrange("p w t -> p (w t)"),
+            )
+            nc.vector.quantize_mx(
+                out=g_codes[:].bitcast(E5M2X4),
+                scales=g_scales[:],
+                in_=g_grp[:].rearrange("p w t -> p (w t)"),
+            )
+            for m in range(M_TILES):
+                cols = slice(m * P, (m + 1) * P)
+                nc.tensor.matmul_mx(
+                    out=acc[m][:],
+                    lhsT=x_codes[:, cols].bitcast(E4M3X4),
+                    lhsT_scale=x_scales[:, cols],
+                    rhs=g_codes[:].bitcast(E5M2X4),
+                    rhs_scale=g_scales[:],
+                    start=(c == 0),
+                    stop=(c == PASSES - 1),
+                )
+            if c == 2:
+                nc.scalar.activation(out=pow2[:], in_=shift_sb[:], func=ACT.Exp, scale=LN2)
+                for m in range(M_TILES):
+                    nc.vector.scalar_tensor_tensor(
+                        out=weight[:, m, :],
+                        in0=sign_sb[:, m, :],
+                        scalar=0.5,
+                        in1=pow2[:, m, :],
+                        op0=ALU.subtract,
+                        op1=ALU.mult,
+                    )
+
+        for m in range(M_TILES):
+            res = w_pool.tile([P, OUT_DIM], F32, name="res%d" % m)
+            nc.vector.scalar_tensor_tensor(
+                out=res[:],
+                in0=acc[m][:],
+                scalar=-2.0 * LN2,
+                in1=weight[:, m, :],
+                op0=ALU.mult,
+                op1=ALU.mult,
+            )
+            nc.sync.dma_start(out=out[m * P : (m + 1) * P, :], in_=res[:])

@@ -2,6 +2,7 @@ from contextlib import ExitStack
 import math
 
 import concourse.mybir as mybir
+from concourse.masks import make_identity
 
 BF16 = mybir.dt.bfloat16
 F32 = mybir.dt.float32
@@ -25,11 +26,17 @@ LN2 = math.log(2.0)
 FLOPS = 2 * TOKENS * IN_DIM * OUT_DIM
 BYTES = 2 * TOKENS * (IN_DIM + OUT_DIM) + 2 * 2 * IN_DIM * OUT_DIM + 4 * IN_DIM * OUT_DIM
 
+RAW_BUFS = 8
+X_VEC = 432
+G_PE = 192
+G_LAST_SCALAR = 392
+W_STEP = 10
 
-def regroup(copy, grouped, raw):
+
+def regroup(copy, grouped, raw, lo, hi):
     copy(
-        out=grouped.rearrange("p (c i) t -> p c t i", i=4),
-        in_=raw.rearrange("p t (c i) -> p c t i", i=4),
+        out=grouped[:, lo:hi, :].rearrange("p (c i) t -> p c t i", i=4),
+        in_=raw[:, :, lo:hi].rearrange("p t (c i) -> p c t i", i=4),
     )
 
 
@@ -38,51 +45,50 @@ def tile_denseshift_kernel(tc, x, shift, sign, bias, grad_out, out):
     x_rows = x.rearrange("(c p j) w -> c p (j w)", p=P, j=PACK)
     g_rows = grad_out.rearrange("(c p j) w -> c p (j w)", p=P, j=PACK)
     with ExitStack() as ctx:
-        raw_pool = ctx.enter_context(tc.tile_pool(name="raw", bufs=8))
+        ctx.enter_context(tc.manual_schedule())
+        raw_pool = ctx.enter_context(tc.tile_pool(name="raw", bufs=RAW_BUFS))
         grp_pool = ctx.enter_context(tc.tile_pool(name="grp", bufs=3))
-        mx_pool = ctx.enter_context(tc.tile_pool(name="mx", bufs=4))
+        mx_pool = ctx.enter_context(tc.tile_pool(name="mx", bufs=3))
         w_pool = ctx.enter_context(tc.tile_pool(name="w", bufs=1))
         psum = ctx.enter_context(tc.psum_pool(name="acc", bufs=1))
+        psum_g = ctx.enter_context(tc.psum_pool(name="pg", bufs=3))
 
         warm = w_pool.tile([P, 1], F32)
         nc.vector.memset(warm[:], 0.0)
         nc.scalar.activation(out=warm[:], in_=warm[:], func=ACT.Exp)
+        ident = w_pool.tile([P, P], BF16)
+        make_identity(nc, ident[:])
 
         acc = [psum.tile([P, OUT_DIM], F32, name="acc%d" % m) for m in range(M_TILES)]
-
         shift_sb = w_pool.tile([P, M_TILES, OUT_DIM], BF16)
         sign_sb = w_pool.tile([P, M_TILES, OUT_DIM], BF16)
         pow2 = w_pool.tile([P, M_TILES, OUT_DIM], F32)
         weight = w_pool.tile([P, M_TILES, OUT_DIM], F32)
 
-        for c in range(PASSES):
-            x_raw = raw_pool.tile([P, PACK, IN_DIM], BF16)
-            g_raw = raw_pool.tile([P, PACK, OUT_DIM], BF16)
-            nc.sync.dma_start(out=x_raw[:].rearrange("p j w -> p (j w)"), in_=x_rows[c])
-            nc.sync.dma_start(out=g_raw[:].rearrange("p j w -> p (j w)"), in_=g_rows[c])
-            if c == 1:
-                nc.sync.dma_start(out=shift_sb[:], in_=shift.rearrange("(m p) n -> p m n", p=P))
-                nc.sync.dma_start(out=sign_sb[:], in_=sign.rearrange("(m p) n -> p m n", p=P))
+        x_raw = {}
+        g_raw = {}
+        x_mx = {}
+        g_grp = {}
 
-            x_grp = grp_pool.tile([P, IN_DIM, PACK], BF16, align_bytes=64)
-            g_grp = grp_pool.tile([P, OUT_DIM, PACK], BF16, align_bytes=64)
-            regroup(nc.vector.tensor_copy, x_grp[:], x_raw[:])
-            regroup(nc.scalar.copy, g_grp[:], g_raw[:])
+        def load_x(c):
+            if c < PASSES:
+                x_raw[c] = raw_pool.tile([P, PACK, IN_DIM], BF16, name="x_raw")
+                nc.sync.dma_start(out=x_raw[c][:].rearrange("p j w -> p (j w)"), in_=x_rows[c])
 
-            x_codes = mx_pool.tile([P, IN_DIM], U32, align_bytes=64)
-            x_scales = mx_pool.tile([P, IN_DIM], U8, align_bytes=64)
-            g_codes = mx_pool.tile([P, OUT_DIM], U32, align_bytes=64)
-            g_scales = mx_pool.tile([P, OUT_DIM], U8, align_bytes=64)
-            nc.vector.quantize_mx(
-                out=x_codes[:].bitcast(E4M3X4),
-                scales=x_scales[:],
-                in_=x_grp[:].rearrange("p w t -> p (w t)"),
-            )
+        def load_g(c):
+            if c < PASSES:
+                g_raw[c] = raw_pool.tile([P, PACK, OUT_DIM], BF16, name="g_raw")
+                nc.sync.dma_start(out=g_raw[c][:].rearrange("p j w -> p (j w)"), in_=g_rows[c])
+
+        def finish(c):
+            g_codes = mx_pool.tile([P, OUT_DIM], U32, align_bytes=64, name="g_codes")
+            g_scales = mx_pool.tile([P, OUT_DIM], U8, align_bytes=64, name="g_scales")
             nc.vector.quantize_mx(
                 out=g_codes[:].bitcast(E5M2X4),
                 scales=g_scales[:],
-                in_=g_grp[:].rearrange("p w t -> p (w t)"),
+                in_=g_grp[c][:].rearrange("p w t -> p (w t)"),
             )
+            x_codes, x_scales = x_mx[c]
             for m in range(M_TILES):
                 cols = slice(m * P, (m + 1) * P)
                 nc.tensor.matmul_mx(
@@ -94,17 +100,63 @@ def tile_denseshift_kernel(tc, x, shift, sign, bias, grad_out, out):
                     start=(c == 0),
                     stop=(c == PASSES - 1),
                 )
-            if c == 2:
-                nc.scalar.activation(out=pow2[:], in_=shift_sb[:], func=ACT.Exp, scale=LN2)
-                for m in range(M_TILES):
-                    nc.vector.scalar_tensor_tensor(
-                        out=weight[:, m, :],
-                        in0=sign_sb[:, m, :],
-                        scalar=0.5,
-                        in1=pow2[:, m, :],
-                        op0=ALU.subtract,
-                        op1=ALU.mult,
-                    )
+
+        for c in range(RAW_BUFS):
+            load_x(c)
+            load_g(c)
+        nc.sync.dma_start(out=shift_sb[:], in_=shift.rearrange("(m p) n -> p m n", p=P))
+        nc.sync.dma_start(out=sign_sb[:], in_=sign.rearrange("(m p) n -> p m n", p=P))
+
+        for c in range(PASSES):
+            last = c == PASSES - 1
+            pg = psum_g.tile([P, G_PE, PACK], BF16, name="pg")
+            for lo in range(0, G_PE, G_PE // 2):
+                hi = lo + G_PE // 2
+                nc.tensor.matmul(
+                    out=pg[:, lo:hi, :].rearrange("p w t -> p t w"),
+                    lhsT=ident[:],
+                    rhs=g_raw[c][:, :, lo:hi],
+                    start=True,
+                    stop=True,
+                )
+
+            x_grp = grp_pool.tile([P, IN_DIM, PACK], BF16, align_bytes=64, name="x_grp")
+            g_grp[c] = grp_pool.tile([P, OUT_DIM, PACK], BF16, align_bytes=64, name="g_grp")
+            regroup(nc.vector.tensor_copy, x_grp, x_raw[c], 0, X_VEC)
+            regroup(nc.scalar.copy, x_grp, x_raw[c], X_VEC, IN_DIM)
+            load_x(c + RAW_BUFS)
+            if c >= 1:
+                finish(c - 1)
+            g_hi = G_LAST_SCALAR if last else OUT_DIM
+            regroup(nc.scalar.copy, g_grp[c], g_raw[c], G_PE, g_hi)
+            if last:
+                regroup(nc.vector.tensor_copy, g_grp[c], g_raw[c], g_hi, OUT_DIM)
+            nc.scalar.copy(out=g_grp[c][:, 0:G_PE, :], in_=pg[:])
+            load_g(c + RAW_BUFS)
+
+            x_codes = mx_pool.tile([P, IN_DIM], U32, align_bytes=64, name="x_codes")
+            x_scales = mx_pool.tile([P, IN_DIM], U8, align_bytes=64, name="x_scales")
+            nc.vector.quantize_mx(
+                out=x_codes[:].bitcast(E4M3X4),
+                scales=x_scales[:],
+                in_=x_grp[:].rearrange("p w t -> p (w t)"),
+            )
+            x_mx[c] = (x_codes, x_scales)
+
+            m = c - W_STEP
+            if 0 <= m < M_TILES:
+                nc.scalar.activation(out=pow2[:, m, :], in_=shift_sb[:, m, :], func=ACT.Exp, scale=LN2)
+            m = c - W_STEP - 1
+            if 0 <= m < M_TILES:
+                nc.vector.scalar_tensor_tensor(
+                    out=weight[:, m, :],
+                    in0=sign_sb[:, m, :],
+                    scalar=0.5,
+                    in1=pow2[:, m, :],
+                    op0=ALU.subtract,
+                    op1=ALU.mult,
+                )
+        finish(PASSES - 1)
 
         for m in range(M_TILES):
             res = w_pool.tile([P, OUT_DIM], F32, name="res%d" % m)

@@ -26,11 +26,12 @@ LN2 = math.log(2.0)
 FLOPS = 2 * TOKENS * IN_DIM * OUT_DIM
 BYTES = 2 * TOKENS * (IN_DIM + OUT_DIM) + 2 * 2 * IN_DIM * OUT_DIM + 4 * IN_DIM * OUT_DIM
 
-RAW_BUFS = 8
+LONG_PASSES = 24
+AHEAD = 4
 X_VEC = 432
 G_PE = 192
 G_LAST_SCALAR = 392
-W_STEP = 10
+ONE_DMA = True
 
 
 def regroup(copy, grouped, raw, lo, hi):
@@ -42,43 +43,73 @@ def regroup(copy, grouped, raw, lo, hi):
 
 def tile_denseshift_kernel(tc, x, shift, sign, bias, grad_out, out):
     nc = tc.nc
-    x_rows = x.rearrange("(c p j) w -> c p (j w)", p=P, j=PACK)
-    g_rows = grad_out.rearrange("(c p j) w -> c p (j w)", p=P, j=PACK)
+    short_rows = {
+        "x": x.rearrange("(c p j) w -> c p (j w)", p=P, j=PACK),
+        "g": grad_out.rearrange("(c p j) w -> c p (j w)", p=P, j=PACK),
+    }
+    long_rows = {
+        "x": x.rearrange("(z r c h k) w -> z c r h (k w)", z=4, r=32, c=4, h=4, k=8),
+        "g": grad_out.rearrange("(z r c h k) w -> z c r h (k w)", z=4, r=32, c=4, h=4, k=8),
+    }
+    groups = [(2 * u, 2) for u in range(LONG_PASSES // 2)] + [(c, 1) for c in range(LONG_PASSES, PASSES)]
+    group_end = dict((first + n - 1, i) for i, (first, n) in enumerate(groups))
+
     with ExitStack() as ctx:
         ctx.enter_context(tc.manual_schedule())
-        raw_pool = ctx.enter_context(tc.tile_pool(name="raw", bufs=RAW_BUFS))
+        raw_pool = ctx.enter_context(tc.tile_pool(name="raw", bufs=AHEAD))
         grp_pool = ctx.enter_context(tc.tile_pool(name="grp", bufs=3))
         mx_pool = ctx.enter_context(tc.tile_pool(name="mx", bufs=3))
         w_pool = ctx.enter_context(tc.tile_pool(name="w", bufs=1))
         psum = ctx.enter_context(tc.psum_pool(name="acc", bufs=1))
         psum_g = ctx.enter_context(tc.psum_pool(name="pg", bufs=3))
 
-        warm = w_pool.tile([P, 1], F32)
-        nc.vector.memset(warm[:], 0.0)
-        nc.scalar.activation(out=warm[:], in_=warm[:], func=ACT.Exp)
-        ident = w_pool.tile([P, P], BF16)
-        make_identity(nc, ident[:])
+        raw = {"x": {}, "g": {}}
+        x_mx = {}
+        g_grp = {}
 
-        acc = [psum.tile([P, OUT_DIM], F32, name="acc%d" % m) for m in range(M_TILES)]
+        def load(which, i):
+            if i >= len(groups):
+                return
+            first, n = groups[i]
+            if n == 1:
+                t = raw_pool.tile([P, PACK, IN_DIM], BF16, name=which + "_short")
+                nc.sync.dma_start(out=t[:].rearrange("p j w -> p (j w)"), in_=short_rows[which][first])
+                raw[which][first] = t
+            else:
+                t = raw_pool.tile([P, 2 * PACK, IN_DIM], BF16, name=which + "_long")
+                src = long_rows[which][i // 4, i % 4]
+                if ONE_DMA:
+                    nc.sync.dma_start(out=t[:].rearrange("p k w -> p (k w)"), in_=src)
+                else:
+                    for h in range(4):
+                        nc.sync.dma_start(out=t[h:P:4].rearrange("p k w -> p (k w)"), in_=src[:, h])
+                raw[which][first] = t[:, 0:PACK, :]
+                raw[which][first + 1] = t[:, PACK : 2 * PACK, :]
+
         shift_sb = w_pool.tile([P, M_TILES, OUT_DIM], BF16)
         sign_sb = w_pool.tile([P, M_TILES, OUT_DIM], BF16)
         pow2 = w_pool.tile([P, M_TILES, OUT_DIM], F32)
         weight = w_pool.tile([P, M_TILES, OUT_DIM], F32)
+        nc.sync.dma_start(out=shift_sb[:], in_=shift.rearrange("(m p) n -> p m n", p=P))
+        nc.sync.dma_start(out=sign_sb[:], in_=sign.rearrange("(m p) n -> p m n", p=P))
+        for i in range(AHEAD):
+            load("x", i)
+            load("g", i)
 
-        x_raw = {}
-        g_raw = {}
-        x_mx = {}
-        g_grp = {}
+        ident = w_pool.tile([P, P], BF16)
+        make_identity(nc, ident[:])
+        acc = [psum.tile([P, OUT_DIM], F32, name="acc%d" % m) for m in range(M_TILES)]
 
-        def load_x(c):
-            if c < PASSES:
-                x_raw[c] = raw_pool.tile([P, PACK, IN_DIM], BF16, name="x_raw")
-                nc.sync.dma_start(out=x_raw[c][:].rearrange("p j w -> p (j w)"), in_=x_rows[c])
-
-        def load_g(c):
-            if c < PASSES:
-                g_raw[c] = raw_pool.tile([P, PACK, OUT_DIM], BF16, name="g_raw")
-                nc.sync.dma_start(out=g_raw[c][:].rearrange("p j w -> p (j w)"), in_=g_rows[c])
+        for m in range(M_TILES):
+            nc.scalar.activation(out=pow2[:, m, :], in_=shift_sb[:, m, :], func=ACT.Exp, scale=LN2)
+            nc.vector.scalar_tensor_tensor(
+                out=weight[:, m, :],
+                in0=sign_sb[:, m, :],
+                scalar=0.5,
+                in1=pow2[:, m, :],
+                op0=ALU.subtract,
+                op1=ALU.mult,
+            )
 
         def finish(c):
             g_codes = mx_pool.tile([P, OUT_DIM], U32, align_bytes=64, name="g_codes")
@@ -101,38 +132,36 @@ def tile_denseshift_kernel(tc, x, shift, sign, bias, grad_out, out):
                     stop=(c == PASSES - 1),
                 )
 
-        for c in range(RAW_BUFS):
-            load_x(c)
-            load_g(c)
-        nc.sync.dma_start(out=shift_sb[:], in_=shift.rearrange("(m p) n -> p m n", p=P))
-        nc.sync.dma_start(out=sign_sb[:], in_=sign.rearrange("(m p) n -> p m n", p=P))
-
         for c in range(PASSES):
             last = c == PASSES - 1
+            x_raw = raw["x"][c]
+            g_raw = raw["g"][c]
             pg = psum_g.tile([P, G_PE, PACK], BF16, name="pg")
             for lo in range(0, G_PE, G_PE // 2):
                 hi = lo + G_PE // 2
                 nc.tensor.matmul(
                     out=pg[:, lo:hi, :].rearrange("p w t -> p t w"),
                     lhsT=ident[:],
-                    rhs=g_raw[c][:, :, lo:hi],
+                    rhs=g_raw[:, :, lo:hi],
                     start=True,
                     stop=True,
                 )
 
             x_grp = grp_pool.tile([P, IN_DIM, PACK], BF16, align_bytes=64, name="x_grp")
             g_grp[c] = grp_pool.tile([P, OUT_DIM, PACK], BF16, align_bytes=64, name="g_grp")
-            regroup(nc.vector.tensor_copy, x_grp, x_raw[c], 0, X_VEC)
-            regroup(nc.scalar.copy, x_grp, x_raw[c], X_VEC, IN_DIM)
-            load_x(c + RAW_BUFS)
+            regroup(nc.vector.tensor_copy, x_grp, x_raw, 0, X_VEC)
+            regroup(nc.scalar.copy, x_grp, x_raw, X_VEC, IN_DIM)
+            if c in group_end:
+                load("x", group_end[c] + AHEAD)
             if c >= 1:
                 finish(c - 1)
             g_hi = G_LAST_SCALAR if last else OUT_DIM
-            regroup(nc.scalar.copy, g_grp[c], g_raw[c], G_PE, g_hi)
+            regroup(nc.scalar.copy, g_grp[c], g_raw, G_PE, g_hi)
             if last:
-                regroup(nc.vector.tensor_copy, g_grp[c], g_raw[c], g_hi, OUT_DIM)
+                regroup(nc.vector.tensor_copy, g_grp[c], g_raw, g_hi, OUT_DIM)
             nc.scalar.copy(out=g_grp[c][:, 0:G_PE, :], in_=pg[:])
-            load_g(c + RAW_BUFS)
+            if c in group_end:
+                load("g", group_end[c] + AHEAD)
 
             x_codes = mx_pool.tile([P, IN_DIM], U32, align_bytes=64, name="x_codes")
             x_scales = mx_pool.tile([P, IN_DIM], U8, align_bytes=64, name="x_scales")
@@ -142,20 +171,6 @@ def tile_denseshift_kernel(tc, x, shift, sign, bias, grad_out, out):
                 in_=x_grp[:].rearrange("p w t -> p (w t)"),
             )
             x_mx[c] = (x_codes, x_scales)
-
-            m = c - W_STEP
-            if 0 <= m < M_TILES:
-                nc.scalar.activation(out=pow2[:, m, :], in_=shift_sb[:, m, :], func=ACT.Exp, scale=LN2)
-            m = c - W_STEP - 1
-            if 0 <= m < M_TILES:
-                nc.vector.scalar_tensor_tensor(
-                    out=weight[:, m, :],
-                    in0=sign_sb[:, m, :],
-                    scalar=0.5,
-                    in1=pow2[:, m, :],
-                    op0=ALU.subtract,
-                    op1=ALU.mult,
-                )
         finish(PASSES - 1)
 
         for m in range(M_TILES):

@@ -36,8 +36,8 @@ ONE_DMA = True
 
 def regroup(copy, grouped, raw, lo, hi):
     copy(
-        out=grouped[:, lo:hi, :].rearrange("p (c i) t -> p c t i", i=4),
-        in_=raw[:, :, lo:hi].rearrange("p t (c i) -> p c t i", i=4),
+        out=grouped[:, lo:hi, :].rearrange("p (c i) t -> p c t i", i=8),
+        in_=raw[:, :, lo:hi].rearrange("p t (c i) -> p c t i", i=8),
     )
 
 

@@ -29,12 +29,22 @@ BYTES = 2 * TOKENS * (IN_DIM + OUT_DIM) + 2 * 2 * IN_DIM * OUT_DIM + 4 * IN_DIM 
 LONG_PASSES = 24
 AHEAD = 4
 X_VEC = 432
-G_PE = 192
-G_LAST_SCALAR = 392
-ONE_DMA = True
+G_PE = 200
+G_LAST_SCALAR = 352
+X_LAST_VEC = 304
+LOOKAHEAD = 1
+S_ORDER = "xgc"
+V_ORDER = "xqq"
+LOAD_ORDER = "xg"
+SPLIT = ""
+TAIL = "c1"
+W_HALVES = False
+GRP_BUFS = 3
 
 
 def regroup(copy, grouped, raw, lo, hi):
+    if hi <= lo:
+        return
     copy(
         out=grouped[:, lo:hi, :].rearrange("p (c i) t -> p c t i", i=8),
         in_=raw[:, :, lo:hi].rearrange("p t (c i) -> p c t i", i=8),
@@ -57,15 +67,16 @@ def tile_denseshift_kernel(tc, x, shift, sign, bias, grad_out, out):
     with ExitStack() as ctx:
         ctx.enter_context(tc.manual_schedule())
         raw_pool = ctx.enter_context(tc.tile_pool(name="raw", bufs=AHEAD))
-        grp_pool = ctx.enter_context(tc.tile_pool(name="grp", bufs=3))
-        mx_pool = ctx.enter_context(tc.tile_pool(name="mx", bufs=3))
+        grp_pool = ctx.enter_context(tc.tile_pool(name="grp", bufs=GRP_BUFS))
+        mx_pool = ctx.enter_context(tc.tile_pool(name="mx", bufs=GRP_BUFS))
         w_pool = ctx.enter_context(tc.tile_pool(name="w", bufs=1))
         psum = ctx.enter_context(tc.psum_pool(name="acc", bufs=1))
-        psum_g = ctx.enter_context(tc.psum_pool(name="pg", bufs=3))
+        psum_g = ctx.enter_context(tc.psum_pool(name="pg", bufs=4))
 
         raw = {"x": {}, "g": {}}
         x_mx = {}
         g_grp = {}
+        pgs = {}
 
         def load(which, i):
             if i >= len(groups):
@@ -77,12 +88,16 @@ def tile_denseshift_kernel(tc, x, shift, sign, bias, grad_out, out):
                 raw[which][first] = t
             else:
                 t = raw_pool.tile([P, 2 * PACK, IN_DIM], BF16, name=which + "_long")
-                src = long_rows[which][i // 4, i % 4]
-                if ONE_DMA:
-                    nc.sync.dma_start(out=t[:].rearrange("p k w -> p (k w)"), in_=src)
+                src = long_rows[which][first // 8, (first // 2) % 4]
+                if which in SPLIT:
+                    half = PACK * IN_DIM
+                    for u in range(2):
+                        nc.sync.dma_start(
+                            out=t[:, u * PACK : (u + 1) * PACK, :].rearrange("p k w -> p (k w)"),
+                            in_=src[:, :, u * half : (u + 1) * half],
+                        )
                 else:
-                    for h in range(4):
-                        nc.sync.dma_start(out=t[h:P:4].rearrange("p k w -> p (k w)"), in_=src[:, h])
+                    nc.sync.dma_start(out=t[:].rearrange("p k w -> p (k w)"), in_=src)
                 raw[which][first] = t[:, 0:PACK, :]
                 raw[which][first + 1] = t[:, PACK : 2 * PACK, :]
 
@@ -90,11 +105,14 @@ def tile_denseshift_kernel(tc, x, shift, sign, bias, grad_out, out):
         sign_sb = w_pool.tile([P, M_TILES, OUT_DIM], BF16)
         pow2 = w_pool.tile([P, M_TILES, OUT_DIM], F32)
         weight = w_pool.tile([P, M_TILES, OUT_DIM], F32)
-        nc.sync.dma_start(out=shift_sb[:], in_=shift.rearrange("(m p) n -> p m n", p=P))
-        nc.sync.dma_start(out=sign_sb[:], in_=sign.rearrange("(m p) n -> p m n", p=P))
+        step = 2 if W_HALVES else M_TILES
+        for m in range(0, M_TILES, step):
+            rows = slice(m * P, (m + step) * P)
+            nc.sync.dma_start(out=shift_sb[:, m : m + step, :], in_=shift[rows, :].rearrange("(m p) n -> p m n", p=P))
+            nc.sync.dma_start(out=sign_sb[:, m : m + step, :], in_=sign[rows, :].rearrange("(m p) n -> p m n", p=P))
         for i in range(AHEAD):
-            load("x", i)
-            load("g", i)
+            for which in LOAD_ORDER:
+                load(which, i)
 
         ident = w_pool.tile([P, P], BF16)
         make_identity(nc, ident[:])
@@ -103,84 +121,113 @@ def tile_denseshift_kernel(tc, x, shift, sign, bias, grad_out, out):
         for m in range(M_TILES):
             nc.scalar.activation(out=pow2[:, m, :], in_=shift_sb[:, m, :], func=ACT.Exp, scale=LN2)
             nc.vector.scalar_tensor_tensor(
-                out=weight[:, m, :],
-                in0=sign_sb[:, m, :],
-                scalar=0.5,
-                in1=pow2[:, m, :],
-                op0=ALU.subtract,
-                op1=ALU.mult,
+                out=weight[:, m, :], in0=sign_sb[:, m, :], scalar=0.5, in1=pow2[:, m, :], op0=ALU.subtract, op1=ALU.mult
             )
 
-        def finish(c):
-            g_codes = mx_pool.tile([P, OUT_DIM], U32, align_bytes=64, name="g_codes")
-            g_scales = mx_pool.tile([P, OUT_DIM], U8, align_bytes=64, name="g_scales")
-            nc.vector.quantize_mx(
-                out=g_codes[:].bitcast(E5M2X4),
-                scales=g_scales[:],
-                in_=g_grp[c][:].rearrange("p w t -> p (w t)"),
-            )
-            x_codes, x_scales = x_mx[c]
-            for m in range(M_TILES):
-                cols = slice(m * P, (m + 1) * P)
-                nc.tensor.matmul_mx(
-                    out=acc[m][:],
-                    lhsT=x_codes[:, cols].bitcast(E4M3X4),
-                    lhsT_scale=x_scales[:, cols],
-                    rhs=g_codes[:].bitcast(E5M2X4),
-                    rhs_scale=g_scales[:],
-                    start=(c == 0),
-                    stop=(c == PASSES - 1),
-                )
-
-        for c in range(PASSES):
-            last = c == PASSES - 1
-            x_raw = raw["x"][c]
-            g_raw = raw["g"][c]
-            pg = psum_g.tile([P, G_PE, PACK], BF16, name="pg")
+        def through_pe(c):
+            if c >= PASSES:
+                return
+            pgs[c] = psum_g.tile([P, G_PE, PACK], BF16, name="pg")
             for lo in range(0, G_PE, G_PE // 2):
                 hi = lo + G_PE // 2
                 nc.tensor.matmul(
-                    out=pg[:, lo:hi, :].rearrange("p w t -> p t w"),
+                    out=pgs[c][:, lo:hi, :].rearrange("p w t -> p t w"),
                     lhsT=ident[:],
-                    rhs=g_raw[:, :, lo:hi],
+                    rhs=raw["g"][c][:, :, lo:hi],
                     start=True,
                     stop=True,
                 )
 
+        def quantize_g(c):
+            g_codes = mx_pool.tile([P, OUT_DIM], U32, align_bytes=64, name="g_codes")
+            g_scales = mx_pool.tile([P, OUT_DIM], U8, align_bytes=64, name="g_scales")
+            nc.vector.quantize_mx(
+                out=g_codes[:].bitcast(E5M2X4), scales=g_scales[:], in_=g_grp[c][:].rearrange("p w t -> p (w t)")
+            )
+            return g_codes, g_scales
+
+        def multiply(c, m, g_codes, g_scales):
+            x_codes, x_scales = x_mx[c]
+            cols = slice(m * P, (m + 1) * P)
+            nc.tensor.matmul_mx(
+                out=acc[m][:],
+                lhsT=x_codes[:, cols].bitcast(E4M3X4),
+                lhsT_scale=x_scales[:, cols],
+                rhs=g_codes[:].bitcast(E5M2X4),
+                rhs_scale=g_scales[:],
+                start=(c == 0),
+                stop=(c == PASSES - 1),
+            )
+
+        def finish(c):
+            g_codes, g_scales = quantize_g(c)
+            for m in range(M_TILES):
+                multiply(c, m, g_codes, g_scales)
+
+        for c in range(LOOKAHEAD):
+            through_pe(c)
+        for c in range(PASSES):
+            last = c == PASSES - 1
+            x_raw = raw["x"][c]
+            g_raw = raw["g"][c]
+            through_pe(c + LOOKAHEAD)
+            pg = pgs[c]
             x_grp = grp_pool.tile([P, IN_DIM, PACK], BF16, align_bytes=64, name="x_grp")
             g_grp[c] = grp_pool.tile([P, OUT_DIM, PACK], BF16, align_bytes=64, name="g_grp")
-            regroup(nc.vector.tensor_copy, x_grp, x_raw, 0, X_VEC)
-            regroup(nc.scalar.copy, x_grp, x_raw, X_VEC, IN_DIM)
-            if c in group_end:
-                load("x", group_end[c] + AHEAD)
-            if c >= 1:
-                finish(c - 1)
-            g_hi = G_LAST_SCALAR if last else OUT_DIM
-            regroup(nc.scalar.copy, g_grp[c], g_raw, G_PE, g_hi)
-            if last:
-                regroup(nc.vector.tensor_copy, g_grp[c], g_raw, g_hi, OUT_DIM)
-            nc.scalar.copy(out=g_grp[c][:, 0:G_PE, :], in_=pg[:])
-            if c in group_end:
-                load("g", group_end[c] + AHEAD)
-
             x_codes = mx_pool.tile([P, IN_DIM], U32, align_bytes=64, name="x_codes")
             x_scales = mx_pool.tile([P, IN_DIM], U8, align_bytes=64, name="x_scales")
-            nc.vector.quantize_mx(
-                out=x_codes[:].bitcast(E4M3X4),
-                scales=x_scales[:],
-                in_=x_grp[:].rearrange("p w t -> p (w t)"),
-            )
             x_mx[c] = (x_codes, x_scales)
-        finish(PASSES - 1)
+            if last and TAIL == "c1":
+                regroup(nc.scalar.copy, g_grp[c], g_raw, G_PE, G_LAST_SCALAR)
+                regroup(nc.vector.tensor_copy, g_grp[c], g_raw, G_LAST_SCALAR, OUT_DIM)
+                nc.scalar.copy(out=g_grp[c][:, 0:G_PE, :], in_=pg[:])
+                finish(c - 1)
+                regroup(nc.vector.tensor_copy, x_grp, x_raw, 0, X_LAST_VEC)
+                regroup(nc.scalar.copy, x_grp, x_raw, X_LAST_VEC, IN_DIM)
+                g_codes, g_scales = quantize_g(c)
+                for m in range(M_TILES):
+                    nc.vector.quantize_mx(
+                        out=x_codes[:, m * P : (m + 1) * P].bitcast(E4M3X4),
+                        scales=x_scales[:, m * P : (m + 1) * P],
+                        in_=x_grp[:, m * P : (m + 1) * P, :].rearrange("p w t -> p (w t)"),
+                    )
+                    multiply(c, m, g_codes, g_scales)
+                continue
+            next_group = group_end[c] + AHEAD if c in group_end else len(groups)
+            swap = TAIL == "c1" and next_group == len(groups) - 1
+            g_hi = G_LAST_SCALAR if last else OUT_DIM
+
+            def s_x():
+                regroup(nc.scalar.copy, x_grp, x_raw, X_VEC, IN_DIM)
+
+            def s_g():
+                regroup(nc.scalar.copy, g_grp[c], g_raw, G_PE, g_hi)
+
+            def s_c():
+                nc.scalar.copy(out=g_grp[c][:, 0:G_PE, :], in_=pg[:])
+
+            s_ops = {"x": s_x, "g": s_g, "c": s_c}
+            if V_ORDER == "qxq" and c >= 1:
+                finish(c - 1)
+            regroup(nc.vector.tensor_copy, x_grp, x_raw, 0, X_VEC)
+            if V_ORDER == "xqq" and c >= 1:
+                finish(c - 1)
+            for o in S_ORDER:
+                s_ops[o]()
+            if last:
+                regroup(nc.vector.tensor_copy, g_grp[c], g_raw, g_hi, OUT_DIM)
+            order = "gx" if swap else LOAD_ORDER
+            for which in order:
+                load(which, next_group)
+            nc.vector.quantize_mx(
+                out=x_codes[:].bitcast(E4M3X4), scales=x_scales[:], in_=x_grp[:].rearrange("p w t -> p (w t)")
+            )
+        if TAIL != "c1":
+            finish(PASSES - 1)
 
         for m in range(M_TILES):
             res = w_pool.tile([P, OUT_DIM], F32, name="res%d" % m)
             nc.vector.scalar_tensor_tensor(
-                out=res[:],
-                in0=acc[m][:],
-                scalar=-2.0 * LN2,
-                in1=weight[:, m, :],
-                op0=ALU.mult,
-                op1=ALU.mult,
+                out=res[:], in0=acc[m][:], scalar=-2.0 * LN2, in1=weight[:, m, :], op0=ALU.mult, op1=ALU.mult
             )
             nc.sync.dma_start(out=out[m * P : (m + 1) * P, :], in_=res[:])

from contextlib import ExitStack
import math

import concourse.mybir as mybir
from concourse.masks import make_identity

BF16 = mybir.dt.bfloat16
F32 = mybir.dt.float32
U32 = mybir.dt.uint32
U8 = mybir.dt.uint8
E4M3X4 = mybir.dt.float8_e4m3fn_x4
E5M2X4 = mybir.dt.float8_e5m2_x4
ALU = mybir.AluOpType
ACT = mybir.ActivationFunctionType

P = 128
PACK = 4
K_PASS = P * PACK
TOKENS = 16384
IN_DIM = 512
OUT_DIM = 512
M_TILES = IN_DIM // P
PASSES = TOKENS // K_PASS
LN2 = math.log(2.0)

FLOPS = 2 * TOKENS * IN_DIM * OUT_DIM
BYTES = 2 * TOKENS * (IN_DIM + OUT_DIM) + 2 * 2 * IN_DIM * OUT_DIM + 4 * IN_DIM * OUT_DIM

LONG_PASSES = 24
AHEAD = 4
X_VEC = 432
G_PE = 200
G_LAST_SCALAR = 352
X_LAST_VEC = 304
LOOKAHEAD = 1
S_ORDER = "xgc"
V_ORDER = "xqq"
LOAD_ORDER = "xg"
SPLIT = ""
TAIL = "c1"
W_HALVES = False
GRP_BUFS = 3


def regroup(copy, grouped, raw, lo, hi):
    if hi <= lo:
        return
    copy(
        out=grouped[:, lo:hi, :].rearrange("p (c i) t -> p c t i", i=8),
        in_=raw[:, :, lo:hi].rearrange("p t (c i) -> p c t i", i=8),
    )


def tile_denseshift_kernel(tc, x, shift, sign, bias, grad_out, out):
    nc = tc.nc
    short_rows = {
        "x": x.rearrange("(c p j) w -> c p (j w)", p=P, j=PACK),
        "g": grad_out.rearrange("(c p j) w -> c p (j w)", p=P, j=PACK),
    }
    long_rows = {
        "x": x.rearrange("(z r c h k) w -> z c r h (k w)", z=4, r=32, c=4, h=4, k=8),
        "g": grad_out.rearrange("(z r c h k) w -> z c r h (k w)", z=4, r=32, c=4, h=4, k=8),
    }
    groups = [(2 * u, 2) for u in range(LONG_PASSES // 2)] + [(c, 1) for c in range(LONG_PASSES, PASSES)]
    group_end = dict((first + n - 1, i) for i, (first, n) in enumerate(groups))

    with ExitStack() as ctx:
        ctx.enter_context(tc.manual_schedule())
        raw_pool = ctx.enter_context(tc.tile_pool(name="raw", bufs=AHEAD))
        grp_pool = ctx.enter_context(tc.tile_pool(name="grp", bufs=GRP_BUFS))
        mx_pool = ctx.enter_context(tc.tile_pool(name="mx", bufs=GRP_BUFS))
        w_pool = ctx.enter_context(tc.tile_pool(name="w", bufs=1))
        psum = ctx.enter_context(tc.psum_pool(name="acc", bufs=1))
        psum_g = ctx.enter_context(tc.psum_pool(name="pg", bufs=4))

        raw = {"x": {}, "g": {}}
        x_mx = {}
        g_grp = {}
        pgs = {}

        def load(which, i):
            if i >= len(groups):
                return
            first, n = groups[i]
            if n == 1:
                t = raw_pool.tile([P, PACK, IN_DIM], BF16, name=which + "_short")
                nc.sync.dma_start(out=t[:].rearrange("p j w -> p (j w)"), in_=short_rows[which][first])
                raw[which][first] = t
            else:
                t = raw_pool.tile([P, 2 * PACK, IN_DIM], BF16, name=which + "_long")
                src = long_rows[which][first // 8, (first // 2) % 4]
                if which in SPLIT:
                    half = PACK * IN_DIM
                    for u in range(2):
                        nc.sync.dma_start(
                            out=t[:, u * PACK : (u + 1) * PACK, :].rearrange("p k w -> p (k w)"),
                            in_=src[:, :, u * half : (u + 1) * half],
                        )
                else:
                    nc.sync.dma_start(out=t[:].rearrange("p k w -> p (k w)"), in_=src)
                raw[which][first] = t[:, 0:PACK, :]
                raw[which][first + 1] = t[:, PACK : 2 * PACK, :]

        shift_sb = w_pool.tile([P, M_TILES, OUT_DIM], BF16)
        sign_sb = w_pool.tile([P, M_TILES, OUT_DIM], BF16)
        pow2 = w_pool.tile([P, M_TILES, OUT_DIM], F32)
        weight = w_pool.tile([P, M_TILES, OUT_DIM], F32)
        step = 2 if W_HALVES else M_TILES
        for m in range(0, M_TILES, step):
            rows = slice(m * P, (m + step) * P)
            nc.sync.dma_start(out=shift_sb[:, m : m + step, :], in_=shift[rows, :].rearrange("(m p) n -> p m n", p=P))
            nc.sync.dma_start(out=sign_sb[:, m : m + step, :], in_=sign[rows, :].rearrange("(m p) n -> p m n", p=P))
        for i in range(AHEAD):
            for which in LOAD_ORDER:
                load(which, i)

        ident = w_pool.tile([P, P], BF16)
        make_identity(nc, ident[:])
        acc = [psum.tile([P, OUT_DIM], F32, name="acc%d" % m) for m in range(M_TILES)]

        for m in range(M_TILES):
            nc.scalar.activation(out=pow2[:, m, :], in_=shift_sb[:, m, :], func=ACT.Exp, scale=LN2)
            nc.vector.scalar_tensor_tensor(
                out=weight[:, m, :], in0=sign_sb[:, m, :], scalar=0.5, in1=pow2[:, m, :], op0=ALU.subtract, op1=ALU.mult
            )

        def through_pe(c):
            if c >= PASSES:
                return
            pgs[c] = psum_g.tile([P, G_PE, PACK], BF16, name="pg")
            for lo in range(0, G_PE, G_PE // 2):
                hi = lo + G_PE // 2
                nc.tensor.matmul(
                    out=pgs[c][:, lo:hi, :].rearrange("p w t -> p t w"),
                    lhsT=ident[:],
                    rhs=raw["g"][c][:, :, lo:hi],
                    start=True,
                    stop=True,
                )

        def quantize_g(c):
            g_codes = mx_pool.tile([P, OUT_DIM], U32, align_bytes=64, name="g_codes")
            g_scales = mx_pool.tile([P, OUT_DIM], U8, align_bytes=64, name="g_scales")
            nc.vector.quantize_mx(
                out=g_codes[:].bitcast(E5M2X4), scales=g_scales[:], in_=g_grp[c][:].rearrange("p w t -> p (w t)")
            )
            return g_codes, g_scales

        def multiply(c, m, g_codes, g_scales):
            x_codes, x_scales = x_mx[c]
            cols = slice(m * P, (m + 1) * P)
            nc.tensor.matmul_mx(
                out=acc[m][:],
                lhsT=x_codes[:, cols].bitcast(E4M3X4),
                lhsT_scale=x_scales[:, cols],
                rhs=g_codes[:].bitcast(E5M2X4),
                rhs_scale=g_scales[:],
                start=(c == 0),
                stop=(c == PASSES - 1),
            )

        def finish(c):
            g_codes, g_scales = quantize_g(c)
            for m in range(M_TILES):
                multiply(c, m, g_codes, g_scales)

        for c in range(LOOKAHEAD):
            through_pe(c)
        for c in range(PASSES):
            last = c == PASSES - 1
            x_raw = raw["x"][c]
            g_raw = raw["g"][c]
            through_pe(c + LOOKAHEAD)
            pg = pgs[c]
            x_grp = grp_pool.tile([P, IN_DIM, PACK], BF16, align_bytes=64, name="x_grp")
            g_grp[c] = grp_pool.tile([P, OUT_DIM, PACK], BF16, align_bytes=64, name="g_grp")
            x_codes = mx_pool.tile([P, IN_DIM], U32, align_bytes=64, name="x_codes")
            x_scales = mx_pool.tile([P, IN_DIM], U8, align_bytes=64, name="x_scales")
            x_mx[c] = (x_codes, x_scales)
            if last and TAIL == "c1":
                regroup(nc.scalar.copy, g_grp[c], g_raw, G_PE, G_LAST_SCALAR)
                regroup(nc.vector.tensor_copy, g_grp[c], g_raw, G_LAST_SCALAR, OUT_DIM)
                nc.scalar.copy(out=g_grp[c][:, 0:G_PE, :], in_=pg[:])
                finish(c - 1)
                regroup(nc.vector.tensor_copy, x_grp, x_raw, 0, X_LAST_VEC)
                regroup(nc.scalar.copy, x_grp, x_raw, X_LAST_VEC, IN_DIM)
                g_codes, g_scales = quantize_g(c)
                for m in range(M_TILES):
                    nc.vector.quantize_mx(
                        out=x_codes[:, m * P : (m + 1) * P].bitcast(E4M3X4),
                        scales=x_scales[:, m * P : (m + 1) * P],
                        in_=x_grp[:, m * P : (m + 1) * P, :].rearrange("p w t -> p (w t)"),
                    )
                    multiply(c, m, g_codes, g_scales)
                continue
            next_group = group_end[c] + AHEAD if c in group_end else len(groups)
            swap = TAIL == "c1" and next_group == len(groups) - 1
            g_hi = G_LAST_SCALAR if last else OUT_DIM

            def s_x():
                regroup(nc.scalar.copy, x_grp, x_raw, X_VEC, IN_DIM)

            def s_g():
                regroup(nc.scalar.copy, g_grp[c], g_raw, G_PE, g_hi)

            def s_c():
                nc.scalar.copy(out=g_grp[c][:, 0:G_PE, :], in_=pg[:])

            s_ops = {"x": s_x, "g": s_g, "c": s_c}
            if V_ORDER == "qxq" and c >= 1:
                finish(c - 1)
            regroup(nc.vector.tensor_copy, x_grp, x_raw, 0, X_VEC)
            if V_ORDER == "xqq" and c >= 1:
                finish(c - 1)
            for o in S_ORDER:
                s_ops[o]()
            if last:
                regroup(nc.vector.tensor_copy, g_grp[c], g_raw, g_hi, OUT_DIM)
            order = "gx" if swap else LOAD_ORDER
            for which in order:
                load(which, next_group)
            nc.vector.quantize_mx(
                out=x_codes[:].bitcast(E4M3X4), scales=x_scales[:], in_=x_grp[:].rearrange("p w t -> p (w t)")
            )
        if TAIL != "c1":
            finish(PASSES - 1)

        for m in range(M_TILES):
            res = w_pool.tile([P, OUT_DIM], F32, name="res%d" % m)
            nc.vector.scalar_tensor_tensor(
                out=res[:], in0=acc[m][:], scalar=-2.0 * LN2, in1=weight[:, m, :], op0=ALU.mult, op1=ALU.mult
            )
            nc.sync.dma_start(out=out[m * P : (m + 1) * P, :], in_=res[:])
